import numpy as np
import ml_dtypes


def mxq(x, axis, fmt="e4m3"):
    dtype, down = {"e4m3": (ml_dtypes.float8_e4m3fn, 7), "e5m2": (ml_dtypes.float8_e5m2, 14)}[fmt]
    v = np.moveaxis(np.asarray(x, np.float32).astype(ml_dtypes.bfloat16).astype(np.float64), axis, -1)
    blocks = v.reshape(v.shape[:-1] + (-1, 32))
    amax = np.abs(blocks).max(-1, keepdims=True)
    byte = np.maximum(np.where(amax > 0, np.frexp(amax)[1] - 1 + 127, 0) - down, 1)
    scale = np.exp2(byte - 127.0)
    codes = (blocks / scale).astype(np.float32).astype(dtype).astype(np.float64)
    return np.moveaxis((codes * scale).reshape(v.shape), -1, axis)


WIDE = False


def mx_kscale(k):
    if not WIDE:
        return np.ones(k)
    levels = np.array([10, -10, 5, -5, 0])
    a = np.random.permutation(np.resize(levels, k // 512 * 4)).reshape(k // 512, 4)
    idx = np.arange(k)
    return np.exp2(a[idx // 512, idx % 128 // 32])


BF16 = ml_dtypes.bfloat16


def bf(x):
    return np.asarray(x, np.float32).astype(BF16)


def f64(x):
    return np.asarray(x).astype(np.float64)


E2M1 = np.array([0.0, 0.5, 1.0, 1.5, 2.0, 3.0, 4.0, 6.0, -0.0, -0.5, -1.0, -1.5, -2.0, -3.0, -4.0, -6.0])


def pack_weight(w, fmt):
    k, n = w.shape
    w = f64(bf(w)).reshape(k // 32, 32, n)
    amax = np.abs(w).max(1)
    if fmt == "e4m3":
        byte = np.frexp(amax)[1] - 1 + 127 - 7
    else:
        mant, ex = np.frexp(amax / 6.0)
        byte = np.where(mant > 0.5, ex, ex - 1) + 127
    byte = np.clip(np.where(amax > 0, byte, 1), 1, 254)
    scaled = (w * np.exp2(127.0 - byte)[:, None, :]).reshape(k, n).astype(np.float32)
    by_word = np.ascontiguousarray(scaled.reshape(k // 512, 128, 4, n).transpose(0, 1, 3, 2))
    if fmt == "e4m3":
        words = by_word.astype(ml_dtypes.float8_e4m3fn).view(np.uint8)
    else:
        c = by_word.astype(ml_dtypes.float4_e2m1fn).view(np.uint8) & 0xF
        words = c[..., 0::2] | (c[..., 1::2] << 4)
    return np.ascontiguousarray(words), np.ascontiguousarray(byte.astype(np.uint8).reshape(k // 512, 16, n))


def unpack_weight(words, scales, fmt):
    g, p, n, _ = words.shape
    if fmt == "e4m3":
        vals = np.ascontiguousarray(words).view(ml_dtypes.float8_e4m3fn).astype(np.float64)
    else:
        nib = np.empty((g, p, n, 4), np.uint8)
        nib[..., 0::2] = words & 0xF
        nib[..., 1::2] = words >> 4
        vals = E2M1[nib]
    vals = vals * np.repeat(np.exp2(scales.astype(np.float64) - 127.0), 8, axis=1)[..., None]
    return vals.transpose(0, 1, 3, 2).reshape(g * 512, n)


N, D, H, HD = 1024, 1024, 16, 72
P = H * HD
HALF = HD // 2
EPS = 1e-6
FMT = "e4m3"


def rms_norm(y):
    ms = np.mean(y * y, axis=-1, keepdims=True) + EPS
    return y * (1.0 / np.sqrt(ms))


def rotate_half(z):
    h = z.shape[-1] // 2
    return np.concatenate([-z[..., h:], z[..., :h]], axis=-1)


def rope_2d(y, cos, sin):
    def ap(z, c, s):
        return z * c[:, None, :] + rotate_half(z) * s[:, None, :]

    return np.concatenate([ap(y[..., :HALF], cos[:, :HALF], sin[:, :HALF]), ap(y[..., HALF:], cos[:, HALF:], sin[:, HALF:])], axis=-1)


def setup_inputs():
    s = mx_kscale(D)
    hidden_states = bf(np.random.standard_normal((N, D)) * s)
    cos = bf(np.random.uniform(-1.0, 1.0, (N, HD)))
    sin = bf(np.random.uniform(-1.0, 1.0, (N, HD)))
    Wq_words, Wq_scales = pack_weight(np.random.standard_normal((D, P)) / np.sqrt(D) / s[:, None], FMT)
    Wk_words, Wk_scales = pack_weight(np.random.standard_normal((D, P)) / np.sqrt(D) / s[:, None], FMT)
    Wv_words, Wv_scales = pack_weight(np.random.standard_normal((D, P)) / np.sqrt(D) / s[:, None], FMT)
    q_scale = bf(1.0 + 0.1 * np.random.standard_normal(HD))
    k_scale = bf(1.0 + 0.1 * np.random.standard_normal(HD))
    return {
        "hidden_states": hidden_states,
        "cos": cos,
        "sin": sin,
        "Wq_words": Wq_words,
        "Wq_scales": Wq_scales,
        "Wk_words": Wk_words,
        "Wk_scales": Wk_scales,
        "Wv_words": Wv_words,
        "Wv_scales": Wv_scales,
        "q_scale": q_scale,
        "k_scale": k_scale,
    }


def reference(hidden_states, cos, sin, Wq_words, Wq_scales, Wk_words, Wk_scales, Wv_words, Wv_scales, q_scale, k_scale):
    x = mxq(f64(hidden_states), 1, "e4m3")
    c, s = f64(cos), f64(sin)
    yq = (x @ unpack_weight(Wq_words, Wq_scales, FMT)).reshape(N, H, HD)
    yk = (x @ unpack_weight(Wk_words, Wk_scales, FMT)).reshape(N, H, HD)
    yv = (x @ unpack_weight(Wv_words, Wv_scales, FMT)).reshape(N, H, HD)
    q = rms_norm(yq) * f64(q_scale)
    k = rms_norm(yk) * f64(k_scale)
    v = rms_norm(yv)
    return rope_2d(q, c, s), rope_2d(k, c, s), v

@@ -1,0 +1,226 @@
+from contextlib import ExitStack
+
+import concourse.mybir as mybir
+from concourse.masks import make_identity
+
+F32 = mybir.dt.float32
+BF16 = mybir.dt.bfloat16
+I32 = mybir.dt.int32
+U32 = mybir.dt.uint32
+U8 = mybir.dt.uint8
+FP8X4 = mybir.dt.float8_e4m3fn_x4
+ALU = mybir.AluOpType
+ACT = mybir.ActivationFunctionType
+
+P = 128
+TOKENS = 1024
+D_MODEL = 1024
+HEADS = 16
+HEAD_DIM = 72
+COLS = HEADS * HEAD_DIM
+EPS = 1e-6
+ROPE_HALF = 18
+
+PACK = 4
+K_PASS = P * PACK
+PASSES = D_MODEL // K_PASS
+PAIRS_PASS = K_PASS // 2
+TOKEN_TILES = TOKENS // P
+BANK_COLS = 512
+PSUM_BANKS = 8
+SLICE_STEP = 64
+PROJECTIONS = 3
+ROTATED = 2
+
+FLOPS = 2 * TOKENS * D_MODEL * PROJECTIONS * COLS
+
+
+def head_windows():
+    windows = []
+    head = 0
+    while head < HEADS:
+        start = head * HEAD_DIM // SLICE_STEP * SLICE_STEP
+        width = max(n for n in (128, 256, 512) if start + n <= COLS)
+        count = min(HEADS - head, (start + width - head * HEAD_DIM) // HEAD_DIM)
+        windows.append((start, width, head, count))
+        head += count
+    return windows
+
+
+def halves(row):
+    return row.rearrange("p (b s i) -> p b s i", s=2, i=ROPE_HALF)
+
+
+def tile_torchgemma4visionattention_pa_kernel(
+    tc,
+    hidden_states,
+    cos,
+    sin,
+    wq_words,
+    wq_scales,
+    wk_words,
+    wk_scales,
+    wv_words,
+    wv_scales,
+    q_scale,
+    k_scale,
+    out_q,
+    out_k,
+    out_v,
+):
+    nc = tc.nc
+    weights = ((wq_words, wq_scales), (wk_words, wk_scales), (wv_words, wv_scales))
+    gains = (q_scale, k_scale)
+    outs = (out_q, out_k, out_v)
+    windows = head_windows()
+
+    with ExitStack() as stack:
+        keep = stack.enter_context(tc.tile_pool(name="keep", bufs=1))
+        stage = stack.enter_context(tc.tile_pool(name="stage", bufs=2))
+        stats = stack.enter_context(tc.tile_pool(name="stats", bufs=6))
+        rows = stack.enter_context(tc.tile_pool(name="rows", bufs=3))
+        psum = stack.enter_context(tc.psum_pool(name="psum", bufs=PSUM_BANKS))
+
+        identity = keep.tile([P, P], F32)
+        make_identity(nc, identity[:])
+        eps = keep.tile([P, 1], F32)
+        nc.vector.memset(eps[:], EPS)
+        squares = keep.tile([P, HEAD_DIM], F32)
+        nc.scalar.activation(out=squares[:, 0:1], in_=eps[:], func=ACT.Sqrt)
+
+        x_rows = keep.tile([P, TOKEN_TILES, D_MODEL], BF16)
+
+        def load_tokens(t):
+            nc.sync.dma_start(out=x_rows[:, t, :], in_=hidden_states[t * P : (t + 1) * P, :])
+
+        w_words = keep.tile([P, PROJECTIONS, PASSES, COLS], U32, align_bytes=64)
+        w_planes = keep.tile([P, PROJECTIONS, COLS], U8, align_bytes=64)
+        nc.vector.memset(w_planes[:].bitcast(I32), 0)
+
+        load_tokens(0)
+        for j, (words, scales) in enumerate(weights):
+            for quadrant in range(4):
+                nc.sync.dma_start(
+                    out=w_planes[32 * quadrant : 32 * quadrant + 4 * PASSES, j, :].bitcast(I32),
+                    in_=scales[:, 4 * quadrant : 4 * quadrant + 4, :].bitcast(I32),
+                )
+            for g in range(PASSES):
+                nc.sync.dma_start(
+                    out=w_words[:, j, g, :].bitcast(I32),
+                    in_=words[g].rearrange("p n t -> p (n t)").bitcast(I32),
+                )
+        for t in range(1, TOKEN_TILES):
+            load_tokens(t)
+
+        cos_rows = keep.tile([P, TOKEN_TILES, HEAD_DIM], BF16)
+        sin_rows = keep.tile([P, TOKEN_TILES, HEAD_DIM], BF16)
+        nc.scalar.dma_start(out=cos_rows[:], in_=cos.rearrange("(t p) f -> p t f", p=P))
+        nc.scalar.dma_start(out=sin_rows[:], in_=sin.rearrange("(t p) f -> p t f", p=P))
+
+        tables = keep.tile([P, TOKEN_TILES, ROTATED, 2, HEAD_DIM], F32)
+        for j in range(ROTATED):
+            gain = keep.tile([P, HEAD_DIM], BF16, name="gain_%d" % j)
+            nc.scalar.dma_start(out=gain[:], in_=gains[j].partition_broadcast(P))
+            nc.vector.tensor_tensor(
+                out=tables[:, :, j, 0, :],
+                in0=cos_rows[:],
+                in1=gain[:].unsqueeze(1).to_broadcast([P, TOKEN_TILES, HEAD_DIM]),
+                op=ALU.mult,
+            )
+            signed_gain = keep.tile([P, HEAD_DIM], F32, name="signed_gain_%d" % j)
+            nc.vector.tensor_copy(out=halves(signed_gain[:])[:, :, 0, :], in_=halves(gain[:])[:, :, 0, :])
+            nc.vector.tensor_scalar_mul(
+                out=halves(signed_gain[:])[:, :, 1, :], in0=halves(gain[:])[:, :, 1, :], scalar1=-1.0
+            )
+            for s in range(2):
+                nc.vector.tensor_tensor(
+                    out=tables[:, :, j, 1, :].rearrange("p t (b s i) -> p t b s i", s=2, i=ROPE_HALF)[:, :, :, s, :],
+                    in0=sin_rows[:].rearrange("p t (b s i) -> p t b s i", s=2, i=ROPE_HALF)[:, :, :, 1 - s, :],
+                    in1=halves(signed_gain[:])[:, :, s, :].unsqueeze(1).to_broadcast([P, TOKEN_TILES, 2, ROPE_HALF]),
+                    op=ALU.mult,
+                )
+
+        x_words = keep.tile([P, TOKEN_TILES, PASSES, P], U32, align_bytes=64)
+        x_planes = keep.tile([P, TOKEN_TILES, PASSES, P], U8, align_bytes=64)
+
+        def quantise_tokens(t):
+            pairs = x_rows[:, t, :].bitcast(F32)
+            flipped = psum.tile([P, PASSES, 2, P], F32, tag="bank")
+            for g in range(PASSES):
+                for u in range(2):
+                    every_second = pairs[:, g * PAIRS_PASS + u : (g + 1) * PAIRS_PASS : 2]
+                    nc.tensor.transpose(flipped[:, g, u, :], every_second, identity[:])
+            grouped = stage.tile([P, PASSES, P, PACK], BF16, align_bytes=64)
+            nc.scalar.copy(out=grouped[:].bitcast(F32), in_=flipped[:].rearrange("p g u r -> p g r u"))
+            nc.vector.quantize_mx(
+                out=x_words[:, t, :, :].rearrange("p g r -> p (g r)").bitcast(FP8X4),
+                scales=x_planes[:, t, :, :].rearrange("p g r -> p (g r)"),
+                in_=grouped[:].rearrange("p g r e -> p (g r e)"),
+            )
+
+        def project(t, j, window):
+            start, width, head0, count = window
+            bank = psum.tile([P, BANK_COLS], F32, tag="bank")
+            for g in range(PASSES):
+                nc.tensor.matmul_mx(
+                    out=bank[:, :width],
+                    lhsT=x_words[:, t, g, :].bitcast(FP8X4),
+                    lhsT_scale=x_planes[:, t, g, :],
+                    rhs=w_words[:, j, g, start : start + width].bitcast(FP8X4),
+                    rhs_scale=w_planes[4 * g : P, j, start : start + width],
+                    start=(g == 0),
+                    stop=(g == PASSES - 1),
+                )
+            first = head0 * HEAD_DIM - start
+            heads = bank[:, first : first + count * HEAD_DIM].rearrange("p (h f) -> p h f", f=HEAD_DIM)
+
+            sum_squares = stats.tile([P, count], F32, tag="sum_squares")
+            for i in range(count):
+                nc.scalar.activation(
+                    out=squares[:], in_=heads[:, i, :], func=ACT.Square, accum_out=sum_squares[:, i : i + 1]
+                )
+            rms = stats.tile([P, count], F32, tag="rms")
+            nc.scalar.activation(out=rms[:], in_=sum_squares[:], func=ACT.Sqrt, scale=1.0 / HEAD_DIM, bias=eps[:])
+            inv_rms = stats.tile([P, count], F32, tag="inv_rms")
+            nc.vector.reciprocal(inv_rms[:], rms[:])
+            return heads, inv_rms
+
+        quantise_tokens(0)
+        for t in range(TOKEN_TILES):
+            if t + 1 < TOKEN_TILES:
+                quantise_tokens(t + 1)
+            for j in range(PROJECTIONS):
+                token_rows = outs[j][t * P : (t + 1) * P].rearrange("p h f -> p (h f)")
+                if j < ROTATED:
+                    terms = rows.tile([P, 2, COLS], F32)
+                    for window in windows:
+                        heads, inv_rms = project(t, j, window)
+                        for i in range(window[3]):
+                            h = window[2] + i
+                            nc.vector.scalar_tensor_tensor(
+                                out=terms[:, :, h * HEAD_DIM : (h + 1) * HEAD_DIM],
+                                in0=heads[:, i, :].unsqueeze(1).to_broadcast([P, 2, HEAD_DIM]),
+                                scalar=inv_rms[:, i : i + 1],
+                                in1=tables[:, t, j, :, :],
+                                op0=ALU.mult,
+                                op1=ALU.mult,
+                            )
+                    stay = halves(terms[:, 0, :])
+                    cross = halves(terms[:, 1, :])
+                    for s in range(2):
+                        nc.gpsimd.tensor_tensor(
+                            out=stay[:, :, s, :], in0=stay[:, :, s, :], in1=cross[:, :, 1 - s, :], op=ALU.add
+                        )
+                    nc.sync.dma_start(out=token_rows, in_=terms[:, 0, :])
+                else:
+                    normed = rows.tile([P, HEADS, HEAD_DIM], F32)
+                    for window in windows:
+                        heads, inv_rms = project(t, j, window)
+                        head0, count = window[2], window[3]
+                        nc.vector.tensor_tensor(
+                            out=normed[:, head0 : head0 + count, :],
+                            in0=heads,
+                            in1=inv_rms[:].unsqueeze(2).to_broadcast([P, count, HEAD_DIM]),
+                            op=ALU.mult,
+                        )
+                    nc.sync.dma_start(out=token_rows, in_=normed[:].rearrange("p h f -> p (h f)"))

@@ -78,26 +78,24 @@ def tile_torchgemma4visionattention_pa_kernel(
         keep = stack.enter_context(tc.tile_pool(name="keep", bufs=1))
         stage = stack.enter_context(tc.tile_pool(name="stage", bufs=2))
         stats = stack.enter_context(tc.tile_pool(name="stats", bufs=6))
-        rows = stack.enter_context(tc.tile_pool(name="rows", bufs=3))
+        rows = stack.enter_context(tc.tile_pool(name="rows", bufs=4))
         psum = stack.enter_context(tc.psum_pool(name="psum", bufs=PSUM_BANKS))
+        stack.enter_context(tc.manual_schedule())
 
         identity = keep.tile([P, P], F32)
         make_identity(nc, identity[:])
         eps = keep.tile([P, 1], F32)
         nc.vector.memset(eps[:], EPS)
         squares = keep.tile([P, HEAD_DIM], F32)
-        nc.scalar.activation(out=squares[:, 0:1], in_=eps[:], func=ACT.Sqrt)
+        nc.scalar.activation(out=squares[:, 0:1], in_=eps[:], func=ACT.Abs_reciprocal_sqrt)
 
         x_rows = keep.tile([P, TOKEN_TILES, D_MODEL], BF16)
-
-        def load_tokens(t):
+        for t in range(TOKEN_TILES):
             nc.sync.dma_start(out=x_rows[:, t, :], in_=hidden_states[t * P : (t + 1) * P, :])
 
         w_words = keep.tile([P, PROJECTIONS, PASSES, COLS], U32, align_bytes=64)
         w_planes = keep.tile([P, PROJECTIONS, COLS], U8, align_bytes=64)
         nc.vector.memset(w_planes[:].bitcast(I32), 0)
-
-        load_tokens(0)
         for j, (words, scales) in enumerate(weights):
             for quadrant in range(4):
                 nc.sync.dma_start(
@@ -109,18 +107,37 @@ def tile_torchgemma4visionattention_pa_kernel(
                     out=w_words[:, j, g, :].bitcast(I32),
                     in_=words[g].rearrange("p n t -> p (n t)").bitcast(I32),
                 )
-        for t in range(1, TOKEN_TILES):
-            load_tokens(t)
 
         cos_rows = keep.tile([P, TOKEN_TILES, HEAD_DIM], BF16)
         sin_rows = keep.tile([P, TOKEN_TILES, HEAD_DIM], BF16)
         nc.scalar.dma_start(out=cos_rows[:], in_=cos.rearrange("(t p) f -> p t f", p=P))
         nc.scalar.dma_start(out=sin_rows[:], in_=sin.rearrange("(t p) f -> p t f", p=P))
-
-        tables = keep.tile([P, TOKEN_TILES, ROTATED, 2, HEAD_DIM], F32)
+        gain_rows = []
         for j in range(ROTATED):
             gain = keep.tile([P, HEAD_DIM], BF16, name="gain_%d" % j)
             nc.scalar.dma_start(out=gain[:], in_=gains[j].partition_broadcast(P))
+            gain_rows.append(gain)
+
+        x_words = keep.tile([P, TOKEN_TILES, PASSES, P], U32, align_bytes=64)
+        x_planes = keep.tile([P, TOKEN_TILES, PASSES, P], U8, align_bytes=64)
+        for t in range(TOKEN_TILES):
+            pairs = x_rows[:, t, :].bitcast(F32)
+            flipped = psum.tile([P, PASSES, 2, P], F32, tag="bank")
+            for g in range(PASSES):
+                for u in range(2):
+                    every_second = pairs[:, g * PAIRS_PASS + u : (g + 1) * PAIRS_PASS : 2]
+                    nc.tensor.transpose(flipped[:, g, u, :], every_second, identity[:])
+            grouped = stage.tile([P, PASSES, P, PACK], BF16, align_bytes=64)
+            nc.scalar.copy(out=grouped[:].bitcast(F32), in_=flipped[:].rearrange("p g u r -> p g r u"))
+            nc.vector.quantize_mx(
+                out=x_words[:, t, :, :].rearrange("p g r -> p (g r)").bitcast(FP8X4),
+                scales=x_planes[:, t, :, :].rearrange("p g r -> p (g r)"),
+                in_=grouped[:].rearrange("p g r e -> p (g r e)"),
+            )
+
+        tables = keep.tile([P, TOKEN_TILES, ROTATED, 2, HEAD_DIM], F32)
+        for j in range(ROTATED):
+            gain = gain_rows[j]
             nc.vector.tensor_tensor(
                 out=tables[:, :, j, 0, :],
                 in0=cos_rows[:],
@@ -140,26 +157,14 @@ def tile_torchgemma4visionattention_pa_kernel(
                     op=ALU.mult,
                 )
 
-        x_words = keep.tile([P, TOKEN_TILES, PASSES, P], U32, align_bytes=64)
-        x_planes = keep.tile([P, TOKEN_TILES, PASSES, P], U8, align_bytes=64)
+        jobs = [(t, j, window) for t in range(TOKEN_TILES) for j in range(PROJECTIONS) for window in windows]
+        heads_of = []
+        sum_squares_of = {}
+        inv_rms_of = {}
+        row_of = {}
 
-        def quantise_tokens(t):
-            pairs = x_rows[:, t, :].bitcast(F32)
-            flipped = psum.tile([P, PASSES, 2, P], F32, tag="bank")
-            for g in range(PASSES):
-                for u in range(2):
-                    every_second = pairs[:, g * PAIRS_PASS + u : (g + 1) * PAIRS_PASS : 2]
-                    nc.tensor.transpose(flipped[:, g, u, :], every_second, identity[:])
-            grouped = stage.tile([P, PASSES, P, PACK], BF16, align_bytes=64)
-            nc.scalar.copy(out=grouped[:].bitcast(F32), in_=flipped[:].rearrange("p g u r -> p g r u"))
-            nc.vector.quantize_mx(
-                out=x_words[:, t, :, :].rearrange("p g r -> p (g r)").bitcast(FP8X4),
-                scales=x_planes[:, t, :, :].rearrange("p g r -> p (g r)"),
-                in_=grouped[:].rearrange("p g r e -> p (g r e)"),
-            )
-
-        def project(t, j, window):
-            start, width, head0, count = window
+        def multiply(n):
+            t, j, (start, width, head0, count) = jobs[n]
             bank = psum.tile([P, BANK_COLS], F32, tag="bank")
             for g in range(PASSES):
                 nc.tensor.matmul_mx(
@@ -173,38 +178,52 @@ def tile_torchgemma4visionattention_pa_kernel(
                 )
             first = head0 * HEAD_DIM - start
             heads = bank[:, first : first + count * HEAD_DIM].rearrange("p (h f) -> p h f", f=HEAD_DIM)
-
-            sum_squares = stats.tile([P, count], F32, tag="sum_squares")
+            heads_of.append(heads)
+            if head0 == 0:
+                sum_squares = stats.tile([P, HEADS], F32)
+                sum_squares_of[(t, j)] = sum_squares
             for i in range(count):
                 nc.scalar.activation(
-                    out=squares[:], in_=heads[:, i, :], func=ACT.Square, accum_out=sum_squares[:, i : i + 1]
+                    out=squares[:],
+                    in_=heads[:, i, :],
+                    func=ACT.Square,
+                    accum_out=sum_squares_of[(t, j)][:, head0 + i : head0 + i + 1],
                 )
-            rms = stats.tile([P, count], F32, tag="rms")
-            nc.scalar.activation(out=rms[:], in_=sum_squares[:], func=ACT.Sqrt, scale=1.0 / HEAD_DIM, bias=eps[:])
-            inv_rms = stats.tile([P, count], F32, tag="inv_rms")
-            nc.vector.reciprocal(inv_rms[:], rms[:])
-            return heads, inv_rms
 
-        quantise_tokens(0)
-        for t in range(TOKEN_TILES):
-            if t + 1 < TOKEN_TILES:
-                quantise_tokens(t + 1)
-            for j in range(PROJECTIONS):
-                token_rows = outs[j][t * P : (t + 1) * P].rearrange("p h f -> p (h f)")
-                if j < ROTATED:
+        def invert(n):
+            t, j, (start, width, head0, count) = jobs[n]
+            if head0 + count == HEADS:
+                inv_rms = stats.tile([P, HEADS], F32)
+                nc.scalar.activation(
+                    out=inv_rms[:],
+                    in_=sum_squares_of[(t, j)][:],
+                    func=ACT.Abs_reciprocal_sqrt,
+                    scale=1.0 / HEAD_DIM,
+                    bias=eps[:],
+                )
+                inv_rms_of[(t, j)] = inv_rms
+
+        def finish(n):
+            t, j, (start, width, head0, count) = jobs[n]
+            heads, inv_rms = heads_of[n], inv_rms_of[(t, j)]
+            last_window = head0 + count == HEADS
+            token_rows = outs[j][t * P : (t + 1) * P].rearrange("p h f -> p (h f)")
+            if j < ROTATED:
+                if head0 == 0:
                     terms = rows.tile([P, 2, COLS], F32)
-                    for window in windows:
-                        heads, inv_rms = project(t, j, window)
-                        for i in range(window[3]):
-                            h = window[2] + i
-                            nc.vector.scalar_tensor_tensor(
-                                out=terms[:, :, h * HEAD_DIM : (h + 1) * HEAD_DIM],
-                                in0=heads[:, i, :].unsqueeze(1).to_broadcast([P, 2, HEAD_DIM]),
-                                scalar=inv_rms[:, i : i + 1],
-                                in1=tables[:, t, j, :, :],
-                                op0=ALU.mult,
-                                op1=ALU.mult,
-                            )
+                    row_of[(t, j)] = terms
+                terms = row_of[(t, j)]
+                for i in range(count):
+                    h = head0 + i
+                    nc.vector.scalar_tensor_tensor(
+                        out=terms[:, :, h * HEAD_DIM : (h + 1) * HEAD_DIM],
+                        in0=heads[:, i, :].unsqueeze(1).to_broadcast([P, 2, HEAD_DIM]),
+                        scalar=inv_rms[:, h : h + 1],
+                        in1=tables[:, t, j, :, :],
+                        op0=ALU.mult,
+                        op1=ALU.mult,
+                    )
+                if last_window:
                     stay = halves(terms[:, 0, :])
                     cross = halves(terms[:, 1, :])
                     for s in range(2):
@@ -212,15 +231,25 @@ def tile_torchgemma4visionattention_pa_kernel(
                             out=stay[:, :, s, :], in0=stay[:, :, s, :], in1=cross[:, :, 1 - s, :], op=ALU.add
                         )
                     nc.sync.dma_start(out=token_rows, in_=terms[:, 0, :])
-                else:
+            else:
+                if head0 == 0:
                     normed = rows.tile([P, HEADS, HEAD_DIM], F32)
-                    for window in windows:
-                        heads, inv_rms = project(t, j, window)
-                        head0, count = window[2], window[3]
-                        nc.vector.tensor_tensor(
-                            out=normed[:, head0 : head0 + count, :],
-                            in0=heads,
-                            in1=inv_rms[:].unsqueeze(2).to_broadcast([P, count, HEAD_DIM]),
-                            op=ALU.mult,
-                        )
+                    row_of[(t, j)] = normed
+                normed = row_of[(t, j)]
+                nc.vector.tensor_tensor(
+                    out=normed[:, head0 : head0 + count, :],
+                    in0=heads,
+                    in1=inv_rms[:, head0 : head0 + count].unsqueeze(2).to_broadcast([P, count, HEAD_DIM]),
+                    op=ALU.mult,
+                )
+                if last_window:
                     nc.sync.dma_start(out=token_rows, in_=normed[:].rearrange("p h f -> p (h f)"))
+
+        finish_lag = len(windows) + 1
+        for n in range(len(jobs) + finish_lag):
+            if n < len(jobs):
+                multiply(n)
+            if 1 <= n <= len(jobs):
+                invert(n - 1)
+            if n >= finish_lag:
+                finish(n - finish_lag)

@@ -227,7 +227,7 @@ def tile_torchgemma4visionattention_pa_kernel(
                     stay = halves(terms[:, 0, :])
                     cross = halves(terms[:, 1, :])
                     for s in range(2):
-                        nc.gpsimd.tensor_tensor(
+                        nc.vector.tensor_tensor(
                             out=stay[:, :, s, :], in0=stay[:, :, s, :], in1=cross[:, :, 1 - s, :], op=ALU.add
                         )
                     nc.sync.dma_start(out=token_rows, in_=terms[:, 0, :])

@@ -78,6 +78,7 @@ def tile_torchgemma4visionattention_pa_kernel(
         keep = stack.enter_context(tc.tile_pool(name="keep", bufs=1))
         stage = stack.enter_context(tc.tile_pool(name="stage", bufs=2))
         stats = stack.enter_context(tc.tile_pool(name="stats", bufs=6))
+        scratch = stack.enter_context(tc.tile_pool(name="scratch", bufs=2))
         rows = stack.enter_context(tc.tile_pool(name="rows", bufs=4))
         psum = stack.enter_context(tc.psum_pool(name="psum", bufs=PSUM_BANKS))
         stack.enter_context(tc.manual_schedule())
@@ -86,8 +87,8 @@ def tile_torchgemma4visionattention_pa_kernel(
         make_identity(nc, identity[:])
         eps = keep.tile([P, 1], F32)
         nc.vector.memset(eps[:], EPS)
-        squares = keep.tile([P, HEAD_DIM], F32)
-        nc.scalar.activation(out=squares[:, 0:1], in_=eps[:], func=ACT.Abs_reciprocal_sqrt)
+        first_call = keep.tile([P, 1], F32)
+        nc.scalar.activation(out=first_call[:], in_=eps[:], func=ACT.Abs_reciprocal_sqrt)
 
         x_rows = keep.tile([P, TOKEN_TILES, D_MODEL], BF16)
         for t in range(TOKEN_TILES):
@@ -159,6 +160,7 @@ def tile_torchgemma4visionattention_pa_kernel(
 
         jobs = [(t, j, window) for t in range(TOKEN_TILES) for j in range(PROJECTIONS) for window in windows]
         heads_of = []
+        squares_of = {}
         sum_squares_of = {}
         inv_rms_of = {}
         row_of = {}
@@ -182,9 +184,11 @@ def tile_torchgemma4visionattention_pa_kernel(
             if head0 == 0:
                 sum_squares = stats.tile([P, HEADS], F32)
                 sum_squares_of[(t, j)] = sum_squares
+                squares = scratch.tile([P, HEADS, HEAD_DIM], F32)
+                squares_of[(t, j)] = squares
             for i in range(count):
                 nc.scalar.activation(
-                    out=squares[:],
+                    out=squares_of[(t, j)][:, head0 + i, :],
                     in_=heads[:, i, :],
                     func=ACT.Square,
                     accum_out=sum_squares_of[(t, j)][:, head0 + i : head0 + i + 1],
@@ -227,7 +231,7 @@ def tile_torchgemma4visionattention_pa_kernel(
                     stay = halves(terms[:, 0, :])
                     cross = halves(terms[:, 1, :])
                     for s in range(2):
-                        nc.vector.tensor_tensor(
+                        nc.gpsimd.tensor_tensor(
                             out=stay[:, :, s, :], in0=stay[:, :, s, :], in1=cross[:, :, 1 - s, :], op=ALU.add
                         )
                     nc.sync.dma_start(out=token_rows, in_=terms[:, 0, :])

@@ -31,6 +31,7 @@ PSUM_BANKS = 8
 SLICE_STEP = 64
 PROJECTIONS = 3
 ROTATED = 2
+GAIN_PITCH = 128
 
 FLOPS = 2 * TOKENS * D_MODEL * PROJECTIONS * COLS
 
@@ -45,6 +46,10 @@ def head_windows():
         windows.append((start, width, head, count))
         head += count
     return windows
+
+
+def by_tile(per_token):
+    return per_token.rearrange("(p t) n -> p t n", t=TOKEN_TILES)
 
 
 def halves(row):
@@ -87,12 +92,10 @@ def tile_torchgemma4visionattention_pa_kernel(
         make_identity(nc, identity[:])
         eps = keep.tile([P, 1], F32)
         nc.vector.memset(eps[:], EPS)
-        first_call = keep.tile([P, 1], F32)
-        nc.scalar.activation(out=first_call[:], in_=eps[:], func=ACT.Abs_reciprocal_sqrt)
 
         x_rows = keep.tile([P, TOKEN_TILES, D_MODEL], BF16)
         for t in range(TOKEN_TILES):
-            nc.sync.dma_start(out=x_rows[:, t, :], in_=hidden_states[t * P : (t + 1) * P, :])
+            nc.sync.dma_start(out=x_rows[:, t, :], in_=by_tile(hidden_states)[:, t, :])
 
         w_words = keep.tile([P, PROJECTIONS, PASSES, COLS], U32, align_bytes=64)
         w_planes = keep.tile([P, PROJECTIONS, COLS], U8, align_bytes=64)
@@ -111,13 +114,17 @@ def tile_torchgemma4visionattention_pa_kernel(
 
         cos_rows = keep.tile([P, TOKEN_TILES, HEAD_DIM], BF16)
         sin_rows = keep.tile([P, TOKEN_TILES, HEAD_DIM], BF16)
-        nc.scalar.dma_start(out=cos_rows[:], in_=cos.rearrange("(t p) f -> p t f", p=P))
-        nc.scalar.dma_start(out=sin_rows[:], in_=sin.rearrange("(t p) f -> p t f", p=P))
-        gain_rows = []
+        nc.scalar.dma_start(out=cos_rows[:], in_=by_tile(cos))
+        nc.scalar.dma_start(out=sin_rows[:], in_=by_tile(sin))
+
+        gain_seed = keep.tile([P, ROTATED, GAIN_PITCH], BF16)
+        nc.vector.memset(gain_seed[:], 0.0)
+        ones = keep.tile([P, P], BF16)
+        nc.vector.memset(ones[:], 1.0)
         for j in range(ROTATED):
-            gain = keep.tile([P, HEAD_DIM], BF16, name="gain_%d" % j)
-            nc.scalar.dma_start(out=gain[:], in_=gains[j].partition_broadcast(P))
-            gain_rows.append(gain)
+            nc.scalar.dma_start(out=gain_seed[0:1, j, :HEAD_DIM], in_=gains[j].unsqueeze(0))
+        first_call = keep.tile([P, 1], F32)
+        nc.scalar.activation(out=first_call[:], in_=eps[:], func=ACT.Abs_reciprocal_sqrt)
 
         x_words = keep.tile([P, TOKEN_TILES, PASSES, P], U32, align_bytes=64)
         x_planes = keep.tile([P, TOKEN_TILES, PASSES, P], U8, align_bytes=64)
@@ -136,19 +143,29 @@ def tile_torchgemma4visionattention_pa_kernel(
                 in_=grouped[:].rearrange("p g r e -> p (g r e)"),
             )
 
+        gain_bank = psum.tile([P, ROTATED, GAIN_PITCH], F32, tag="bank")
+        nc.tensor.matmul(
+            out=gain_bank[:].rearrange("p j f -> p (j f)"),
+            lhsT=ones[:],
+            rhs=gain_seed[:].rearrange("p j f -> p (j f)"),
+            start=True,
+            stop=True,
+        )
+        gain_rows = keep.tile([P, ROTATED, GAIN_PITCH], F32)
+        nc.scalar.copy(out=gain_rows[:], in_=gain_bank[:])
         tables = keep.tile([P, TOKEN_TILES, ROTATED, 2, HEAD_DIM], F32)
         for j in range(ROTATED):
-            gain = gain_rows[j]
+            gain = gain_rows[:, j, :HEAD_DIM]
             nc.vector.tensor_tensor(
                 out=tables[:, :, j, 0, :],
                 in0=cos_rows[:],
-                in1=gain[:].unsqueeze(1).to_broadcast([P, TOKEN_TILES, HEAD_DIM]),
+                in1=gain.unsqueeze(1).to_broadcast([P, TOKEN_TILES, HEAD_DIM]),
                 op=ALU.mult,
             )
             signed_gain = keep.tile([P, HEAD_DIM], F32, name="signed_gain_%d" % j)
-            nc.vector.tensor_copy(out=halves(signed_gain[:])[:, :, 0, :], in_=halves(gain[:])[:, :, 0, :])
+            nc.vector.tensor_copy(out=halves(signed_gain[:])[:, :, 0, :], in_=halves(gain)[:, :, 0, :])
             nc.vector.tensor_scalar_mul(
-                out=halves(signed_gain[:])[:, :, 1, :], in0=halves(gain[:])[:, :, 1, :], scalar1=-1.0
+                out=halves(signed_gain[:])[:, :, 1, :], in0=halves(gain)[:, :, 1, :], scalar1=-1.0
             )
             for s in range(2):
                 nc.vector.tensor_tensor(
@@ -211,7 +228,7 @@ def tile_torchgemma4visionattention_pa_kernel(
             t, j, (start, width, head0, count) = jobs[n]
             heads, inv_rms = heads_of[n], inv_rms_of[(t, j)]
             last_window = head0 + count == HEADS
-            token_rows = outs[j][t * P : (t + 1) * P].rearrange("p h f -> p (h f)")
+            token_rows = by_tile(outs[j].rearrange("n h f -> n (h f)"))[:, t, :]
             if j < ROTATED:
                 if head0 == 0:
                     terms = rows.tile([P, 2, COLS], F32)

@@ -31,6 +31,7 @@ PSUM_BANKS = 8
 SLICE_STEP = 64
 PROJECTIONS = 3
 ROTATED = 2
+TILE_GROUP = 2
 GAIN_PITCH = 128
 
 FLOPS = 2 * TOKENS * D_MODEL * PROJECTIONS * COLS
@@ -175,7 +176,13 @@ def tile_torchgemma4visionattention_pa_kernel(
                     op=ALU.mult,
                 )
 
-        jobs = [(t, j, window) for t in range(TOKEN_TILES) for j in range(PROJECTIONS) for window in windows]
+        projections = [
+            (t, j)
+            for first in range(0, TOKEN_TILES, TILE_GROUP)
+            for j in range(PROJECTIONS)
+            for t in range(first, first + TILE_GROUP)
+        ]
+        jobs = [(t, j, window) for t, j in projections for window in windows]
         heads_of = []
         squares_of = {}
         sum_squares_of = {}
@@ -263,8 +270,10 @@ def tile_torchgemma4visionattention_pa_kernel(
                     in1=inv_rms[:, head0 : head0 + count].unsqueeze(2).to_broadcast([P, count, HEAD_DIM]),
                     op=ALU.mult,
                 )
-                if last_window:
-                    nc.sync.dma_start(out=token_rows, in_=normed[:].rearrange("p h f -> p (h f)"))
+                nc.sync.dma_start(
+                    out=token_rows[:, head0 * HEAD_DIM : (head0 + count) * HEAD_DIM],
+                    in_=normed[:, head0 : head0 + count, :].rearrange("p h f -> p (h f)"),
+                )
 
         finish_lag = len(windows) + 1
         for n in range(len(jobs) + finish_lag):

@@ -176,12 +176,12 @@ def tile_torchgemma4visionattention_pa_kernel(
                     op=ALU.mult,
                 )
 
-        projections = [
-            (t, j)
-            for first in range(0, TOKEN_TILES, TILE_GROUP)
-            for j in range(PROJECTIONS)
-            for t in range(first, first + TILE_GROUP)
-        ]
+        projections = []
+        for first in range(0, TOKEN_TILES + TILE_GROUP, TILE_GROUP):
+            if first < TOKEN_TILES:
+                projections.extend((t, j) for j in range(ROTATED) for t in range(first, first + TILE_GROUP))
+            if first >= TILE_GROUP:
+                projections.extend((t, ROTATED) for t in range(first - TILE_GROUP, first))
         jobs = [(t, j, window) for t, j in projections for window in windows]
         heads_of = []
         squares_of = {}

@@ -33,6 +33,8 @@ PROJECTIONS = 3
 ROTATED = 2
 TILE_GROUP = 2
 GAIN_PITCH = 128
+PLAIN_START = 2
+MAX_WINDOW_HEADS = BANK_COLS // HEAD_DIM
 
 FLOPS = 2 * TOKENS * D_MODEL * PROJECTIONS * COLS
 
@@ -84,8 +86,9 @@ def tile_torchgemma4visionattention_pa_kernel(
         keep = stack.enter_context(tc.tile_pool(name="keep", bufs=1))
         stage = stack.enter_context(tc.tile_pool(name="stage", bufs=2))
         stats = stack.enter_context(tc.tile_pool(name="stats", bufs=6))
-        scratch = stack.enter_context(tc.tile_pool(name="scratch", bufs=2))
+        scratch = stack.enter_context(tc.tile_pool(name="scratch", bufs=4))
         rows = stack.enter_context(tc.tile_pool(name="rows", bufs=4))
+        plain_rows = stack.enter_context(tc.tile_pool(name="plain_rows", bufs=8))
         psum = stack.enter_context(tc.psum_pool(name="psum", bufs=PSUM_BANKS))
         stack.enter_context(tc.manual_schedule())
 
@@ -176,18 +179,29 @@ def tile_torchgemma4visionattention_pa_kernel(
                     op=ALU.mult,
                 )
 
-        projections = []
-        for first in range(0, TOKEN_TILES + TILE_GROUP, TILE_GROUP):
-            if first < TOKEN_TILES:
-                projections.extend((t, j) for j in range(ROTATED) for t in range(first, first + TILE_GROUP))
-            if first >= TILE_GROUP:
-                projections.extend((t, ROTATED) for t in range(first - TILE_GROUP, first))
-        jobs = [(t, j, window) for t, j in projections for window in windows]
+        rotated = [
+            (t, j)
+            for first in range(0, TOKEN_TILES, TILE_GROUP)
+            for j in range(ROTATED)
+            for t in range(first, first + TILE_GROUP)
+        ]
+        plain = [(t, ROTATED, window) for t in range(TOKEN_TILES) for window in windows]
+        jobs = []
+        for i, (t, j) in enumerate(rotated):
+            jobs.extend((t, j, window) for window in windows)
+            if i >= PLAIN_START:
+                jobs.append(plain[i - PLAIN_START])
+        jobs.extend(plain[len(rotated) - PLAIN_START :])
         heads_of = []
-        squares_of = {}
         sum_squares_of = {}
         inv_rms_of = {}
         row_of = {}
+
+        def norm_group(n):
+            t, j, (start, width, head0, count) = jobs[n]
+            if j < ROTATED:
+                return (t, j, 0), 0, HEADS
+            return (t, j, head0), head0, count
 
         def multiply(n):
             t, j, (start, width, head0, count) = jobs[n]
@@ -205,36 +219,36 @@ def tile_torchgemma4visionattention_pa_kernel(
             first = head0 * HEAD_DIM - start
             heads = bank[:, first : first + count * HEAD_DIM].rearrange("p (h f) -> p h f", f=HEAD_DIM)
             heads_of.append(heads)
-            if head0 == 0:
+            key, group_head0, group_count = norm_group(n)
+            if head0 == group_head0:
                 sum_squares = stats.tile([P, HEADS], F32)
-                sum_squares_of[(t, j)] = sum_squares
-                squares = scratch.tile([P, HEADS, HEAD_DIM], F32)
-                squares_of[(t, j)] = squares
+                sum_squares_of[key] = sum_squares
+            squares = scratch.tile([P, MAX_WINDOW_HEADS, HEAD_DIM], F32)
             for i in range(count):
                 nc.scalar.activation(
-                    out=squares_of[(t, j)][:, head0 + i, :],
+                    out=squares[:, i, :],
                     in_=heads[:, i, :],
                     func=ACT.Square,
-                    accum_out=sum_squares_of[(t, j)][:, head0 + i : head0 + i + 1],
+                    accum_out=sum_squares_of[key][:, head0 + i : head0 + i + 1],
                 )
 
         def invert(n):
             t, j, (start, width, head0, count) = jobs[n]
-            if head0 + count == HEADS:
+            key, group_head0, group_count = norm_group(n)
+            if head0 + count == group_head0 + group_count:
                 inv_rms = stats.tile([P, HEADS], F32)
                 nc.scalar.activation(
-                    out=inv_rms[:],
-                    in_=sum_squares_of[(t, j)][:],
+                    out=inv_rms[:, group_head0 : group_head0 + group_count],
+                    in_=sum_squares_of[key][:, group_head0 : group_head0 + group_count],
                     func=ACT.Abs_reciprocal_sqrt,
                     scale=1.0 / HEAD_DIM,
                     bias=eps[:],
                 )
-                inv_rms_of[(t, j)] = inv_rms
+                inv_rms_of[key] = inv_rms
 
         def finish(n):
             t, j, (start, width, head0, count) = jobs[n]
-            heads, inv_rms = heads_of[n], inv_rms_of[(t, j)]
-            last_window = head0 + count == HEADS
+            heads, inv_rms = heads_of[n], inv_rms_of[norm_group(n)[0]]
             token_rows = by_tile(outs[j].rearrange("n h f -> n (h f)"))[:, t, :]
             if j < ROTATED:
                 if head0 == 0:
@@ -251,35 +265,44 @@ def tile_torchgemma4visionattention_pa_kernel(
                         op0=ALU.mult,
                         op1=ALU.mult,
                     )
-                if last_window:
+                if head0 + count == HEADS:
                     stay = halves(terms[:, 0, :])
                     cross = halves(terms[:, 1, :])
                     for s in range(2):
                         nc.gpsimd.tensor_tensor(
                             out=stay[:, :, s, :], in0=stay[:, :, s, :], in1=cross[:, :, 1 - s, :], op=ALU.add
                         )
-                    nc.sync.dma_start(out=token_rows, in_=terms[:, 0, :])
             else:
-                if head0 == 0:
-                    normed = rows.tile([P, HEADS, HEAD_DIM], F32)
-                    row_of[(t, j)] = normed
-                normed = row_of[(t, j)]
+                normed = plain_rows.tile([P, MAX_WINDOW_HEADS, HEAD_DIM], F32)
                 nc.vector.tensor_tensor(
-                    out=normed[:, head0 : head0 + count, :],
+                    out=normed[:, :count, :],
                     in0=heads,
                     in1=inv_rms[:, head0 : head0 + count].unsqueeze(2).to_broadcast([P, count, HEAD_DIM]),
                     op=ALU.mult,
                 )
                 nc.sync.dma_start(
                     out=token_rows[:, head0 * HEAD_DIM : (head0 + count) * HEAD_DIM],
-                    in_=normed[:, head0 : head0 + count, :].rearrange("p h f -> p (h f)"),
+                    in_=normed[:, :count, :].rearrange("p h f -> p (h f)"),
                 )
 
-        finish_lag = len(windows) + 1
-        for n in range(len(jobs) + finish_lag):
+        def store_rotated(n):
+            t, j, (start, width, head0, count) = jobs[n]
+            if j < ROTATED and head0 + count == HEADS:
+                nc.sync.dma_start(
+                    out=by_tile(outs[j].rearrange("n h f -> n (h f)"))[:, t, :], in_=row_of[(t, j)][:, 0, :]
+                )
+
+        rotated_lag = len(windows) + 1
+        plain_lag = 2
+        store_lag = rotated_lag + 4
+        for n in range(len(jobs) + store_lag):
             if n < len(jobs):
                 multiply(n)
             if 1 <= n <= len(jobs):
                 invert(n - 1)
-            if n >= finish_lag:
-                finish(n - finish_lag)
+            if 0 <= n - rotated_lag < len(jobs) and jobs[n - rotated_lag][1] < ROTATED:
+                finish(n - rotated_lag)
+            if 0 <= n - plain_lag < len(jobs) and jobs[n - plain_lag][1] == ROTATED:
+                finish(n - plain_lag)
+            if 0 <= n - store_lag:
+                store_rotated(n - store_lag)

@@ -191,6 +191,7 @@ def tile_torchgemma4visionattention_pa_kernel(
             jobs.extend((t, j, window) for window in windows)
             if i >= PLAIN_START:
                 jobs.append(plain[i - PLAIN_START])
+        final_run = len(jobs)
         jobs.extend(plain[len(rotated) - PLAIN_START :])
         heads_of = []
         sum_squares_of = {}
@@ -274,12 +275,21 @@ def tile_torchgemma4visionattention_pa_kernel(
                         )
             else:
                 normed = plain_rows.tile([P, MAX_WINDOW_HEADS, HEAD_DIM], F32)
-                nc.vector.tensor_tensor(
-                    out=normed[:, :count, :],
-                    in0=heads,
-                    in1=inv_rms[:, head0 : head0 + count].unsqueeze(2).to_broadcast([P, count, HEAD_DIM]),
-                    op=ALU.mult,
-                )
+                if n < final_run:
+                    for i in range(count):
+                        nc.scalar.activation(
+                            out=normed[:, i, :],
+                            in_=heads[:, i, :],
+                            func=ACT.Copy,
+                            scale=inv_rms[:, head0 + i : head0 + i + 1],
+                        )
+                else:
+                    nc.vector.tensor_tensor(
+                        out=normed[:, :count, :],
+                        in0=heads,
+                        in1=inv_rms[:, head0 : head0 + count].unsqueeze(2).to_broadcast([P, count, HEAD_DIM]),
+                        op=ALU.mult,
+                    )
                 nc.sync.dma_start(
                     out=token_rows[:, head0 * HEAD_DIM : (head0 + count) * HEAD_DIM],
                     in_=normed[:, :count, :].rearrange("p h f -> p (h f)"),

@@ -275,7 +275,7 @@ def tile_torchgemma4visionattention_pa_kernel(
                         )
             else:
                 normed = plain_rows.tile([P, MAX_WINDOW_HEADS, HEAD_DIM], F32)
-                if n < final_run:
+                if n < final_run and head0 == windows[1][2]:
                     for i in range(count):
                         nc.scalar.activation(
                             out=normed[:, i, :],

@@ -33,6 +33,7 @@ PROJECTIONS = 3
 ROTATED = 2
 TILE_GROUP = 2
 GAIN_PITCH = 128
+FINE_PROJECTIONS = 2
 PLAIN_START = 2
 MAX_WINDOW_HEADS = BANK_COLS // HEAD_DIM
 
@@ -200,9 +201,19 @@ def tile_torchgemma4visionattention_pa_kernel(
 
         def norm_group(n):
             t, j, (start, width, head0, count) = jobs[n]
-            if j < ROTATED:
+            if j < ROTATED and (t, j) != rotated[0]:
                 return (t, j, 0), 0, HEADS
             return (t, j, head0), head0, count
+
+        def added_columns(n):
+            t, j, (start, width, head0, count) = jobs[n]
+            if j == ROTATED:
+                return None
+            if (t, j) in rotated[-FINE_PROJECTIONS:]:
+                return slice(head0 * HEAD_DIM, (head0 + count) * HEAD_DIM)
+            if head0 + count == HEADS:
+                return slice(0, COLS)
+            return None
 
         def multiply(n):
             t, j, (start, width, head0, count) = jobs[n]
@@ -266,9 +277,10 @@ def tile_torchgemma4visionattention_pa_kernel(
                         op0=ALU.mult,
                         op1=ALU.mult,
                     )
-                if head0 + count == HEADS:
-                    stay = halves(terms[:, 0, :])
-                    cross = halves(terms[:, 1, :])
+                cols = added_columns(n)
+                if cols is not None:
+                    stay = halves(terms[:, 0, cols])
+                    cross = halves(terms[:, 1, cols])
                     for s in range(2):
                         nc.gpsimd.tensor_tensor(
                             out=stay[:, :, s, :], in0=stay[:, :, s, :], in1=cross[:, :, 1 - s, :], op=ALU.add
@@ -297,9 +309,10 @@ def tile_torchgemma4visionattention_pa_kernel(
 
         def store_rotated(n):
             t, j, (start, width, head0, count) = jobs[n]
-            if j < ROTATED and head0 + count == HEADS:
+            cols = added_columns(n)
+            if cols is not None:
                 nc.sync.dma_start(
-                    out=by_tile(outs[j].rearrange("n h f -> n (h f)"))[:, t, :], in_=row_of[(t, j)][:, 0, :]
+                    out=by_tile(outs[j].rearrange("n h f -> n (h f)"))[:, t, cols], in_=row_of[(t, j)][:, 0, cols]
                 )
 
         rotated_lag = len(windows) + 1

@@ -35,6 +35,7 @@ TILE_GROUP = 2
 GAIN_PITCH = 128
 FINE_PROJECTIONS = 2
 PLAIN_START = 2
+QUANTISE_AHEAD = 5
 MAX_WINDOW_HEADS = BANK_COLS // HEAD_DIM
 
 FLOPS = 2 * TOKENS * D_MODEL * PROJECTIONS * COLS
@@ -99,23 +100,36 @@ def tile_torchgemma4visionattention_pa_kernel(
         nc.vector.memset(eps[:], EPS)
 
         x_rows = keep.tile([P, TOKEN_TILES, D_MODEL], BF16)
-        for t in range(TOKEN_TILES):
-            nc.sync.dma_start(out=x_rows[:, t, :], in_=by_tile(hidden_states)[:, t, :])
-
         w_words = keep.tile([P, PROJECTIONS, PASSES, COLS], U32, align_bytes=64)
         w_planes = keep.tile([P, PROJECTIONS, COLS], U8, align_bytes=64)
         nc.vector.memset(w_planes[:].bitcast(I32), 0)
-        for j, (words, scales) in enumerate(weights):
+
+        def load_tokens(t):
+            nc.sync.dma_start(out=x_rows[:, t, :], in_=by_tile(hidden_states)[:, t, :])
+
+        def load_weights(j):
+            words, scales = weights[j]
             for quadrant in range(4):
                 nc.sync.dma_start(
                     out=w_planes[32 * quadrant : 32 * quadrant + 4 * PASSES, j, :].bitcast(I32),
                     in_=scales[:, 4 * quadrant : 4 * quadrant + 4, :].bitcast(I32),
                 )
-            for g in range(PASSES):
-                nc.sync.dma_start(
-                    out=w_words[:, j, g, :].bitcast(I32),
-                    in_=words[g].rearrange("p n t -> p (n t)").bitcast(I32),
-                )
+            for piece in (slice(0, BANK_COLS), slice(BANK_COLS, COLS)):
+                for g in range(PASSES):
+                    nc.sync.dma_start(
+                        out=w_words[:, j, g, piece].bitcast(I32),
+                        in_=words[g, :, piece, :].rearrange("p n t -> p (n t)").bitcast(I32),
+                    )
+
+        for t in range(TILE_GROUP):
+            load_tokens(t)
+        for j in range(ROTATED):
+            load_weights(j)
+        for t in range(TILE_GROUP, 2 * TILE_GROUP):
+            load_tokens(t)
+        load_weights(ROTATED)
+        for t in range(2 * TILE_GROUP, TOKEN_TILES):
+            load_tokens(t)
 
         cos_rows = keep.tile([P, TOKEN_TILES, HEAD_DIM], BF16)
         sin_rows = keep.tile([P, TOKEN_TILES, HEAD_DIM], BF16)
@@ -133,20 +147,33 @@ def tile_torchgemma4visionattention_pa_kernel(
 
         x_words = keep.tile([P, TOKEN_TILES, PASSES, P], U32, align_bytes=64)
         x_planes = keep.tile([P, TOKEN_TILES, PASSES, P], U8, align_bytes=64)
-        for t in range(TOKEN_TILES):
+        flipped_of = {}
+        grouped_of = {}
+
+        def flip(t):
             pairs = x_rows[:, t, :].bitcast(F32)
             flipped = psum.tile([P, PASSES, 2, P], F32, tag="bank")
             for g in range(PASSES):
                 for u in range(2):
                     every_second = pairs[:, g * PAIRS_PASS + u : (g + 1) * PAIRS_PASS : 2]
                     nc.tensor.transpose(flipped[:, g, u, :], every_second, identity[:])
+            flipped_of[t] = flipped
+
+        def regroup(t):
             grouped = stage.tile([P, PASSES, P, PACK], BF16, align_bytes=64)
-            nc.scalar.copy(out=grouped[:].bitcast(F32), in_=flipped[:].rearrange("p g u r -> p g r u"))
+            nc.scalar.copy(out=grouped[:].bitcast(F32), in_=flipped_of[t][:].rearrange("p g u r -> p g r u"))
+            grouped_of[t] = grouped
+
+        def quantise(t):
             nc.vector.quantize_mx(
                 out=x_words[:, t, :, :].rearrange("p g r -> p (g r)").bitcast(FP8X4),
                 scales=x_planes[:, t, :, :].rearrange("p g r -> p (g r)"),
-                in_=grouped[:].rearrange("p g r e -> p (g r e)"),
+                in_=grouped_of[t][:].rearrange("p g r e -> p (g r e)"),
             )
+
+        for step in (flip, regroup, quantise):
+            for t in range(TILE_GROUP):
+                step(t)
 
         gain_bank = psum.tile([P, ROTATED, GAIN_PITCH], F32, tag="bank")
         nc.tensor.matmul(
@@ -318,13 +345,26 @@ def tile_torchgemma4visionattention_pa_kernel(
         rotated_lag = len(windows) + 1
         plain_lag = 2
         store_lag = rotated_lag + 4
+        first_use = {}
+        for n, (t, j, window) in enumerate(jobs):
+            first_use.setdefault(t, n)
+        ends = [n + rotated_lag for n, (t, j, window) in enumerate(jobs) if j < ROTATED and window == windows[-1]]
+        quantise_in = {}
+        for t in range(TILE_GROUP, TOKEN_TILES):
+            quantise_in.setdefault(max(n for n in ends if n <= first_use[t] - QUANTISE_AHEAD), []).append(t)
         for n in range(len(jobs) + store_lag):
             if n < len(jobs):
                 multiply(n)
+            for t in quantise_in.get(n + 2, []):
+                flip(t)
             if 1 <= n <= len(jobs):
                 invert(n - 1)
+            for t in quantise_in.get(n + 1, []):
+                regroup(t)
             if 0 <= n - rotated_lag < len(jobs) and jobs[n - rotated_lag][1] < ROTATED:
                 finish(n - rotated_lag)
+            for t in quantise_in.get(n, []):
+                quantise(t)
             if 0 <= n - plain_lag < len(jobs) and jobs[n - plain_lag][1] == ROTATED:
                 finish(n - plain_lag)
             if 0 <= n - store_lag:

@@ -35,7 +35,7 @@ TILE_GROUP = 2
 GAIN_PITCH = 128
 FINE_PROJECTIONS = 2
 PLAIN_START = 2
-QUANTISE_AHEAD = 5
+EARLY_TILES = 4
 MAX_WINDOW_HEADS = BANK_COLS // HEAD_DIM
 
 FLOPS = 2 * TOKENS * D_MODEL * PROJECTIONS * COLS
@@ -86,7 +86,7 @@ def tile_torchgemma4visionattention_pa_kernel(
 
     with ExitStack() as stack:
         keep = stack.enter_context(tc.tile_pool(name="keep", bufs=1))
-        stage = stack.enter_context(tc.tile_pool(name="stage", bufs=2))
+        stage = stack.enter_context(tc.tile_pool(name="stage", bufs=4))
         stats = stack.enter_context(tc.tile_pool(name="stats", bufs=6))
         scratch = stack.enter_context(tc.tile_pool(name="scratch", bufs=4))
         rows = stack.enter_context(tc.tile_pool(name="rows", bufs=4))
@@ -121,15 +121,13 @@ def tile_torchgemma4visionattention_pa_kernel(
                         in_=words[g, :, piece, :].rearrange("p n t -> p (n t)").bitcast(I32),
                     )
 
-        for t in range(TILE_GROUP):
+        for t in range(EARLY_TILES):
             load_tokens(t)
-        for j in range(ROTATED):
+        load_weights(0)
+        for t in range(EARLY_TILES, TOKEN_TILES):
+            load_tokens(t)
+        for j in range(1, PROJECTIONS):
             load_weights(j)
-        for t in range(TILE_GROUP, 2 * TILE_GROUP):
-            load_tokens(t)
-        load_weights(ROTATED)
-        for t in range(2 * TILE_GROUP, TOKEN_TILES):
-            load_tokens(t)
 
         cos_rows = keep.tile([P, TOKEN_TILES, HEAD_DIM], BF16)
         sin_rows = keep.tile([P, TOKEN_TILES, HEAD_DIM], BF16)
@@ -172,7 +170,7 @@ def tile_torchgemma4visionattention_pa_kernel(
             )
 
         for step in (flip, regroup, quantise):
-            for t in range(TILE_GROUP):
+            for t in range(EARLY_TILES):
                 step(t)
 
         gain_bank = psum.tile([P, ROTATED, GAIN_PITCH], F32, tag="bank")
@@ -345,26 +343,22 @@ def tile_torchgemma4visionattention_pa_kernel(
         rotated_lag = len(windows) + 1
         plain_lag = 2
         store_lag = rotated_lag + 4
-        first_use = {}
-        for n, (t, j, window) in enumerate(jobs):
-            first_use.setdefault(t, n)
-        ends = [n + rotated_lag for n, (t, j, window) in enumerate(jobs) if j < ROTATED and window == windows[-1]]
-        quantise_in = {}
-        for t in range(TILE_GROUP, TOKEN_TILES):
-            quantise_in.setdefault(max(n for n in ends if n <= first_use[t] - QUANTISE_AHEAD), []).append(t)
+        first_add = len(windows) - 1 + rotated_lag
+        flip_in = {first_add - 1 - (TOKEN_TILES - t): t for t in range(EARLY_TILES, TOKEN_TILES)}
         for n in range(len(jobs) + store_lag):
             if n < len(jobs):
                 multiply(n)
-            for t in quantise_in.get(n + 2, []):
-                flip(t)
+            if n in flip_in:
+                flip(flip_in[n])
             if 1 <= n <= len(jobs):
                 invert(n - 1)
-            for t in quantise_in.get(n + 1, []):
-                regroup(t)
+            if n - 1 in flip_in:
+                regroup(flip_in[n - 1])
+            if n == first_add:
+                for t in range(EARLY_TILES, TOKEN_TILES):
+                    quantise(t)
             if 0 <= n - rotated_lag < len(jobs) and jobs[n - rotated_lag][1] < ROTATED:
                 finish(n - rotated_lag)
-            for t in quantise_in.get(n, []):
-                quantise(t)
             if 0 <= n - plain_lag < len(jobs) and jobs[n - plain_lag][1] == ROTATED:
                 finish(n - plain_lag)
             if 0 <= n - store_lag:

@@ -159,7 +159,11 @@ def tile_torchgemma4visionattention_pa_kernel(
 
         def regroup(t):
             grouped = stage.tile([P, PASSES, P, PACK], BF16, align_bytes=64)
-            nc.scalar.copy(out=grouped[:].bitcast(F32), in_=flipped_of[t][:].rearrange("p g u r -> p g r u"))
+            side_by_side = flipped_of[t][:].rearrange("p g u r -> p g r u")
+            if t < EARLY_TILES:
+                nc.scalar.copy(out=grouped[:].bitcast(F32), in_=side_by_side)
+            else:
+                nc.vector.tensor_copy(out=grouped[:].bitcast(F32), in_=side_by_side)
             grouped_of[t] = grouped
 
         def quantise(t):
@@ -345,6 +349,7 @@ def tile_torchgemma4visionattention_pa_kernel(
         store_lag = rotated_lag + 4
         first_add = len(windows) - 1 + rotated_lag
         flip_in = {first_add - 1 - (TOKEN_TILES - t): t for t in range(EARLY_TILES, TOKEN_TILES)}
+        early_finish = len(windows) - 1
         for n in range(len(jobs) + store_lag):
             if n < len(jobs):
                 multiply(n)
@@ -352,12 +357,13 @@ def tile_torchgemma4visionattention_pa_kernel(
                 flip(flip_in[n])
             if 1 <= n <= len(jobs):
                 invert(n - 1)
+            if 0 <= n - plain_lag < early_finish:
+                finish(n - plain_lag)
             if n - 1 in flip_in:
                 regroup(flip_in[n - 1])
-            if n == first_add:
-                for t in range(EARLY_TILES, TOKEN_TILES):
-                    quantise(t)
-            if 0 <= n - rotated_lag < len(jobs) and jobs[n - rotated_lag][1] < ROTATED:
+            if n - 2 in flip_in:
+                quantise(flip_in[n - 2])
+            if early_finish <= n - rotated_lag < len(jobs) and jobs[n - rotated_lag][1] < ROTATED:
                 finish(n - rotated_lag)
             if 0 <= n - plain_lag < len(jobs) and jobs[n - plain_lag][1] == ROTATED:
                 finish(n - plain_lag)

from contextlib import ExitStack

import concourse.mybir as mybir
from concourse.masks import make_identity

F32 = mybir.dt.float32
BF16 = mybir.dt.bfloat16
I32 = mybir.dt.int32
U32 = mybir.dt.uint32
U8 = mybir.dt.uint8
FP8X4 = mybir.dt.float8_e4m3fn_x4
ALU = mybir.AluOpType
ACT = mybir.ActivationFunctionType

P = 128
TOKENS = 1024
D_MODEL = 1024
HEADS = 16
HEAD_DIM = 72
COLS = HEADS * HEAD_DIM
EPS = 1e-6
ROPE_HALF = 18

PACK = 4
K_PASS = P * PACK
PASSES = D_MODEL // K_PASS
PAIRS_PASS = K_PASS // 2
TOKEN_TILES = TOKENS // P
BANK_COLS = 512
PSUM_BANKS = 8
SLICE_STEP = 64
PROJECTIONS = 3
ROTATED = 2
TILE_GROUP = 2
GAIN_PITCH = 128
FINE_PROJECTIONS = 2
PLAIN_START = 2
EARLY_TILES = 4
MAX_WINDOW_HEADS = BANK_COLS // HEAD_DIM

FLOPS = 2 * TOKENS * D_MODEL * PROJECTIONS * COLS


def head_windows():
    windows = []
    head = 0
    while head < HEADS:
        start = head * HEAD_DIM // SLICE_STEP * SLICE_STEP
        width = max(n for n in (128, 256, 512) if start + n <= COLS)
        count = min(HEADS - head, (start + width - head * HEAD_DIM) // HEAD_DIM)
        windows.append((start, width, head, count))
        head += count
    return windows


def by_tile(per_token):
    return per_token.rearrange("(p t) n -> p t n", t=TOKEN_TILES)


def halves(row):
    return row.rearrange("p (b s i) -> p b s i", s=2, i=ROPE_HALF)


def tile_torchgemma4visionattention_pa_kernel(
    tc,
    hidden_states,
    cos,
    sin,
    wq_words,
    wq_scales,
    wk_words,
    wk_scales,
    wv_words,
    wv_scales,
    q_scale,
    k_scale,
    out_q,
    out_k,
    out_v,
):
    nc = tc.nc
    weights = ((wq_words, wq_scales), (wk_words, wk_scales), (wv_words, wv_scales))
    gains = (q_scale, k_scale)
    outs = (out_q, out_k, out_v)
    windows = head_windows()

    with ExitStack() as stack:
        keep = stack.enter_context(tc.tile_pool(name="keep", bufs=1))
        stage = stack.enter_context(tc.tile_pool(name="stage", bufs=4))
        stats = stack.enter_context(tc.tile_pool(name="stats", bufs=6))
        scratch = stack.enter_context(tc.tile_pool(name="scratch", bufs=4))
        rows = stack.enter_context(tc.tile_pool(name="rows", bufs=4))
        plain_rows = stack.enter_context(tc.tile_pool(name="plain_rows", bufs=8))
        psum = stack.enter_context(tc.psum_pool(name="psum", bufs=PSUM_BANKS))
        stack.enter_context(tc.manual_schedule())

        identity = keep.tile([P, P], F32)
        make_identity(nc, identity[:])
        eps = keep.tile([P, 1], F32)
        nc.vector.memset(eps[:], EPS)

        x_rows = keep.tile([P, TOKEN_TILES, D_MODEL], BF16)
        w_words = keep.tile([P, PROJECTIONS, PASSES, COLS], U32, align_bytes=64)
        w_planes = keep.tile([P, PROJECTIONS, COLS], U8, align_bytes=64)
        nc.vector.memset(w_planes[:].bitcast(I32), 0)

        def load_tokens(t):
            nc.sync.dma_start(out=x_rows[:, t, :], in_=by_tile(hidden_states)[:, t, :])

        def load_weights(j):
            words, scales = weights[j]
            for quadrant in range(4):
                nc.sync.dma_start(
                    out=w_planes[32 * quadrant : 32 * quadrant + 4 * PASSES, j, :].bitcast(I32),
                    in_=scales[:, 4 * quadrant : 4 * quadrant + 4, :].bitcast(I32),
                )
            for piece in (slice(0, BANK_COLS), slice(BANK_COLS, COLS)):
                for g in range(PASSES):
                    nc.sync.dma_start(
                        out=w_words[:, j, g, piece].bitcast(I32),
                        in_=words[g, :, piece, :].rearrange("p n t -> p (n t)").bitcast(I32),
                    )

        for t in range(EARLY_TILES):
            load_tokens(t)
        load_weights(0)
        for t in range(EARLY_TILES, TOKEN_TILES):
            load_tokens(t)
        for j in range(1, PROJECTIONS):
            load_weights(j)

        cos_rows = keep.tile([P, TOKEN_TILES, HEAD_DIM], BF16)
        sin_rows = keep.tile([P, TOKEN_TILES, HEAD_DIM], BF16)
        nc.scalar.dma_start(out=cos_rows[:], in_=by_tile(cos))
        nc.scalar.dma_start(out=sin_rows[:], in_=by_tile(sin))

        gain_seed = keep.tile([P, ROTATED, GAIN_PITCH], BF16)
        nc.vector.memset(gain_seed[:], 0.0)
        ones = keep.tile([P, P], BF16)
        nc.vector.memset(ones[:], 1.0)
        for j in range(ROTATED):
            nc.scalar.dma_start(out=gain_seed[0:1, j, :HEAD_DIM], in_=gains[j].unsqueeze(0))
        first_call = keep.tile([P, 1], F32)
        nc.scalar.activation(out=first_call[:], in_=eps[:], func=ACT.Abs_reciprocal_sqrt)

        x_words = keep.tile([P, TOKEN_TILES, PASSES, P], U32, align_bytes=64)
        x_planes = keep.tile([P, TOKEN_TILES, PASSES, P], U8, align_bytes=64)
        flipped_of = {}
        grouped_of = {}

        def flip(t):
            pairs = x_rows[:, t, :].bitcast(F32)
            flipped = psum.tile([P, PASSES, 2, P], F32, tag="bank")
            for g in range(PASSES):
                for u in range(2):
                    every_second = pairs[:, g * PAIRS_PASS + u : (g + 1) * PAIRS_PASS : 2]
                    nc.tensor.transpose(flipped[:, g, u, :], every_second, identity[:])
            flipped_of[t] = flipped

        def regroup(t):
            grouped = stage.tile([P, PASSES, P, PACK], BF16, align_bytes=64)
            side_by_side = flipped_of[t][:].rearrange("p g u r -> p g r u")
            if t < EARLY_TILES:
                nc.scalar.copy(out=grouped[:].bitcast(F32), in_=side_by_side)
            else:
                nc.vector.tensor_copy(out=grouped[:].bitcast(F32), in_=side_by_side)
            grouped_of[t] = grouped

        def quantise(t):
            nc.vector.quantize_mx(
                out=x_words[:, t, :, :].rearrange("p g r -> p (g r)").bitcast(FP8X4),
                scales=x_planes[:, t, :, :].rearrange("p g r -> p (g r)"),
                in_=grouped_of[t][:].rearrange("p g r e -> p (g r e)"),
            )

        for step in (flip, regroup, quantise):
            for t in range(EARLY_TILES):
                step(t)

        gain_bank = psum.tile([P, ROTATED, GAIN_PITCH], F32, tag="bank")
        nc.tensor.matmul(
            out=gain_bank[:].rearrange("p j f -> p (j f)"),
            lhsT=ones[:],
            rhs=gain_seed[:].rearrange("p j f -> p (j f)"),
            start=True,
            stop=True,
        )
        gain_rows = keep.tile([P, ROTATED, GAIN_PITCH], F32)
        nc.scalar.copy(out=gain_rows[:], in_=gain_bank[:])
        tables = keep.tile([P, TOKEN_TILES, ROTATED, 2, HEAD_DIM], F32)
        for j in range(ROTATED):
            gain = gain_rows[:, j, :HEAD_DIM]
            nc.vector.tensor_tensor(
                out=tables[:, :, j, 0, :],
                in0=cos_rows[:],
                in1=gain.unsqueeze(1).to_broadcast([P, TOKEN_TILES, HEAD_DIM]),
                op=ALU.mult,
            )
            signed_gain = keep.tile([P, HEAD_DIM], F32, name="signed_gain_%d" % j)
            nc.vector.tensor_copy(out=halves(signed_gain[:])[:, :, 0, :], in_=halves(gain)[:, :, 0, :])
            nc.vector.tensor_scalar_mul(
                out=halves(signed_gain[:])[:, :, 1, :], in0=halves(gain)[:, :, 1, :], scalar1=-1.0
            )
            for s in range(2):
                nc.vector.tensor_tensor(
                    out=tables[:, :, j, 1, :].rearrange("p t (b s i) -> p t b s i", s=2, i=ROPE_HALF)[:, :, :, s, :],
                    in0=sin_rows[:].rearrange("p t (b s i) -> p t b s i", s=2, i=ROPE_HALF)[:, :, :, 1 - s, :],
                    in1=halves(signed_gain[:])[:, :, s, :].unsqueeze(1).to_broadcast([P, TOKEN_TILES, 2, ROPE_HALF]),
                    op=ALU.mult,
                )

        rotated = [
            (t, j)
            for first in range(0, TOKEN_TILES, TILE_GROUP)
            for j in range(ROTATED)
            for t in range(first, first + TILE_GROUP)
        ]
        plain = [(t, ROTATED, window) for t in range(TOKEN_TILES) for window in windows]
        jobs = []
        for i, (t, j) in enumerate(rotated):
            jobs.extend((t, j, window) for window in windows)
            if i >= PLAIN_START:
                jobs.append(plain[i - PLAIN_START])
        final_run = len(jobs)
        jobs.extend(plain[len(rotated) - PLAIN_START :])
        heads_of = []
        sum_squares_of = {}
        inv_rms_of = {}
        row_of = {}

        def norm_group(n):
            t, j, (start, width, head0, count) = jobs[n]
            if j < ROTATED and (t, j) != rotated[0]:
                return (t, j, 0), 0, HEADS
            return (t, j, head0), head0, count

        def added_columns(n):
            t, j, (start, width, head0, count) = jobs[n]
            if j == ROTATED:
                return None
            if (t, j) in rotated[-FINE_PROJECTIONS:]:
                return slice(head0 * HEAD_DIM, (head0 + count) * HEAD_DIM)
            if head0 + count == HEADS:
                return slice(0, COLS)
            return None

        def multiply(n):
            t, j, (start, width, head0, count) = jobs[n]
            bank = psum.tile([P, BANK_COLS], F32, tag="bank")
            for g in range(PASSES):
                nc.tensor.matmul_mx(
                    out=bank[:, :width],
                    lhsT=x_words[:, t, g, :].bitcast(FP8X4),
                    lhsT_scale=x_planes[:, t, g, :],
                    rhs=w_words[:, j, g, start : start + width].bitcast(FP8X4),
                    rhs_scale=w_planes[4 * g : P, j, start : start + width],
                    start=(g == 0),
                    stop=(g == PASSES - 1),
                )
            first = head0 * HEAD_DIM - start
            heads = bank[:, first : first + count * HEAD_DIM].rearrange("p (h f) -> p h f", f=HEAD_DIM)
            heads_of.append(heads)
            key, group_head0, group_count = norm_group(n)
            if head0 == group_head0:
                sum_squares = stats.tile([P, HEADS], F32)
                sum_squares_of[key] = sum_squares
            squares = scratch.tile([P, MAX_WINDOW_HEADS, HEAD_DIM], F32)
            for i in range(count):
                nc.scalar.activation(
                    out=squares[:, i, :],
                    in_=heads[:, i, :],
                    func=ACT.Square,
                    accum_out=sum_squares_of[key][:, head0 + i : head0 + i + 1],
                )

        def invert(n):
            t, j, (start, width, head0, count) = jobs[n]
            key, group_head0, group_count = norm_group(n)
            if head0 + count == group_head0 + group_count:
                inv_rms = stats.tile([P, HEADS], F32)
                nc.scalar.activation(
                    out=inv_rms[:, group_head0 : group_head0 + group_count],
                    in_=sum_squares_of[key][:, group_head0 : group_head0 + group_count],
                    func=ACT.Abs_reciprocal_sqrt,
                    scale=1.0 / HEAD_DIM,
                    bias=eps[:],
                )
                inv_rms_of[key] = inv_rms

        def finish(n):
            t, j, (start, width, head0, count) = jobs[n]
            heads, inv_rms = heads_of[n], inv_rms_of[norm_group(n)[0]]
            token_rows = by_tile(outs[j].rearrange("n h f -> n (h f)"))[:, t, :]
            if j < ROTATED:
                if head0 == 0:
                    terms = rows.tile([P, 2, COLS], F32)
                    row_of[(t, j)] = terms
                terms = row_of[(t, j)]
                for i in range(count):
                    h = head0 + i
                    nc.vector.scalar_tensor_tensor(
                        out=terms[:, :, h * HEAD_DIM : (h + 1) * HEAD_DIM],
                        in0=heads[:, i, :].unsqueeze(1).to_broadcast([P, 2, HEAD_DIM]),
                        scalar=inv_rms[:, h : h + 1],
                        in1=tables[:, t, j, :, :],
                        op0=ALU.mult,
                        op1=ALU.mult,
                    )
                cols = added_columns(n)
                if cols is not None:
                    stay = halves(terms[:, 0, cols])
                    cross = halves(terms[:, 1, cols])
                    for s in range(2):
                        nc.gpsimd.tensor_tensor(
                            out=stay[:, :, s, :], in0=stay[:, :, s, :], in1=cross[:, :, 1 - s, :], op=ALU.add
                        )
            else:
                normed = plain_rows.tile([P, MAX_WINDOW_HEADS, HEAD_DIM], F32)
                if n < final_run and head0 == windows[1][2]:
                    for i in range(count):
                        nc.scalar.activation(
                            out=normed[:, i, :],
                            in_=heads[:, i, :],
                            func=ACT.Copy,
                            scale=inv_rms[:, head0 + i : head0 + i + 1],
                        )
                else:
                    nc.vector.tensor_tensor(
                        out=normed[:, :count, :],
                        in0=heads,
                        in1=inv_rms[:, head0 : head0 + count].unsqueeze(2).to_broadcast([P, count, HEAD_DIM]),
                        op=ALU.mult,
                    )
                nc.sync.dma_start(
                    out=token_rows[:, head0 * HEAD_DIM : (head0 + count) * HEAD_DIM],
                    in_=normed[:, :count, :].rearrange("p h f -> p (h f)"),
                )

        def store_rotated(n):
            t, j, (start, width, head0, count) = jobs[n]
            cols = added_columns(n)
            if cols is not None:
                nc.sync.dma_start(
                    out=by_tile(outs[j].rearrange("n h f -> n (h f)"))[:, t, cols], in_=row_of[(t, j)][:, 0, cols]
                )

        rotated_lag = len(windows) + 1
        plain_lag = 2
        store_lag = rotated_lag + 4
        first_add = len(windows) - 1 + rotated_lag
        flip_in = {first_add - 1 - (TOKEN_TILES - t): t for t in range(EARLY_TILES, TOKEN_TILES)}
        early_finish = len(windows) - 1
        for n in range(len(jobs) + store_lag):
            if n < len(jobs):
                multiply(n)
            if n in flip_in:
                flip(flip_in[n])
            if 1 <= n <= len(jobs):
                invert(n - 1)
            if 0 <= n - plain_lag < early_finish:
                finish(n - plain_lag)
            if n - 1 in flip_in:
                regroup(flip_in[n - 1])
            if n - 2 in flip_in:
                quantise(flip_in[n - 2])
            if early_finish <= n - rotated_lag < len(jobs) and jobs[n - rotated_lag][1] < ROTATED:
                finish(n - rotated_lag)
            if 0 <= n - plain_lag < len(jobs) and jobs[n - plain_lag][1] == ROTATED:
                finish(n - plain_lag)
            if 0 <= n - store_lag:
                store_rotated(n - store_lag)
